import numpy as np
import ml_dtypes


def mxq(x, axis, fmt="e4m3"):
    dtype, down = {"e4m3": (ml_dtypes.float8_e4m3fn, 7), "e5m2": (ml_dtypes.float8_e5m2, 14)}[fmt]
    v = np.moveaxis(np.asarray(x, np.float32).astype(ml_dtypes.bfloat16).astype(np.float64), axis, -1)
    blocks = v.reshape(v.shape[:-1] + (-1, 32))
    amax = np.abs(blocks).max(-1, keepdims=True)
    byte = np.maximum(np.where(amax > 0, np.frexp(amax)[1] - 1 + 127, 0) - down, 1)
    scale = np.exp2(byte - 127.0)
    codes = (blocks / scale).astype(np.float32).astype(dtype).astype(np.float64)
    return np.moveaxis((codes * scale).reshape(v.shape), -1, axis)


WIDE = False


def mx_kscale(k):
    if not WIDE:
        return np.ones(k)
    levels = np.array([10, -10, 5, -5, 0])
    a = np.random.permutation(np.resize(levels, k // 512 * 4)).reshape(k // 512, 4)
    idx = np.arange(k)
    return np.exp2(a[idx // 512, idx % 128 // 32])


BF16 = ml_dtypes.bfloat16


def bf(x):
    return np.asarray(x, np.float32).astype(BF16)


def f64(x):
    return np.asarray(x).astype(np.float64)


E2M1 = np.array([0.0, 0.5, 1.0, 1.5, 2.0, 3.0, 4.0, 6.0, -0.0, -0.5, -1.0, -1.5, -2.0, -3.0, -4.0, -6.0])


def pack_weight(w, fmt):
    k, n = w.shape
    w = f64(bf(w)).reshape(k // 32, 32, n)
    amax = np.abs(w).max(1)
    if fmt == "e4m3":
        byte = np.frexp(amax)[1] - 1 + 127 - 7
    else:
        mant, ex = np.frexp(amax / 6.0)
        byte = np.where(mant > 0.5, ex, ex - 1) + 127
    byte = np.clip(np.where(amax > 0, byte, 1), 1, 254)
    scaled = (w * np.exp2(127.0 - byte)[:, None, :]).reshape(k, n).astype(np.float32)
    by_word = np.ascontiguousarray(scaled.reshape(k // 512, 128, 4, n).transpose(0, 1, 3, 2))
    if fmt == "e4m3":
        words = by_word.astype(ml_dtypes.float8_e4m3fn).view(np.uint8)
    else:
        c = by_word.astype(ml_dtypes.float4_e2m1fn).view(np.uint8) & 0xF
        words = c[..., 0::2] | (c[..., 1::2] << 4)
    return np.ascontiguousarray(words), np.ascontiguousarray(byte.astype(np.uint8).reshape(k // 512, 16, n))


def unpack_weight(words, scales, fmt):
    g, p, n, _ = words.shape
    if fmt == "e4m3":
        vals = np.ascontiguousarray(words).view(ml_dtypes.float8_e4m3fn).astype(np.float64)
    else:
        nib = np.empty((g, p, n, 4), np.uint8)
        nib[..., 0::2] = words & 0xF
        nib[..., 1::2] = words >> 4
        vals = E2M1[nib]
    vals = vals * np.repeat(np.exp2(scales.astype(np.float64) - 127.0), 8, axis=1)[..., None]
    return vals.transpose(0, 1, 3, 2).reshape(g * 512, n)


E, D, H, C = 512, 5632, 512, 128


def silu(v):
    return v / (1.0 + np.exp(-v))


def setup_inputs():
    s = mx_kscale(D)
    t = mx_kscale(H)
    node_embed = bf(np.random.standard_normal((E, D)) * s)
    x_edge_c = bf(np.random.standard_normal((E, H)) * t)
    ori = bf(np.random.standard_normal((E, D)) * s)
    W1_words, W1_scales = pack_weight(np.random.standard_normal((D, H)) * 1.0 / np.sqrt(D) / s[:, None], "e4m3")
    b1 = bf(np.random.standard_normal(H) * 0.3)
    W2_words, W2_scales = pack_weight(np.random.standard_normal((H, D)) * 1.5 / np.sqrt(H) / t[:, None], "e4m3")
    b2 = bf(np.random.standard_normal(D) * 0.3)
    return {
        "node_embed": node_embed,
        "x_edge_c": x_edge_c,
        "ori": ori,
        "W1_words": W1_words,
        "W1_scales": W1_scales,
        "b1": b1,
        "W2_words": W2_words,
        "W2_scales": W2_scales,
        "b2": b2,
        "edge_num": E,
    }


def reference(node_embed, x_edge_c, ori, W1_words, W1_scales, b1, W2_words, W2_scales, b2, edge_num):
    x = np.concatenate([f64(node_embed), f64(ori)], axis=0)
    h = silu((mxq(x, 1, "e4m3") @ unpack_weight(W1_words, W1_scales, "e4m3")) + f64(b1))
    h = (h.reshape(2, edge_num, H) * f64(x_edge_c).reshape(1, edge_num, H)).reshape(-1, H)
    y = silu((mxq(h, 1, "e4m3") @ unpack_weight(W2_words, W2_scales, "e4m3")) + f64(b2))
    y = y.reshape(2 * edge_num, -1, C)
    return y[:edge_num] + y[edge_num:]

@@ -1,0 +1,321 @@
+from contextlib import ExitStack
+
+import concourse.mybir as mybir
+from concourse.masks import make_identity
+
+F32 = mybir.dt.float32
+BF16 = mybir.dt.bfloat16
+I32 = mybir.dt.int32
+U32 = mybir.dt.uint32
+U8 = mybir.dt.uint8
+FP8X4 = mybir.dt.float8_e4m3fn_x4
+SILU = mybir.ActivationFunctionType.Silu
+ADD = mybir.AluOpType.add
+MULT = mybir.AluOpType.mult
+
+P = 128
+PACK = 4
+K_PASS = P * PACK
+EDGES, D, H = 512, 5632, 512
+N_TILE = 512
+ROUNDS = EDGES // P
+SLICES = D // K_PASS
+UNITS = ROUNDS * SLICES
+X_CHUNKS = 4
+X_CHUNK = D // X_CHUNKS
+X_RUN = 2
+B1_ROW = SLICES
+BIAS_ROWS = SLICES + 1
+
+LAG_COPY_X = 1
+LAG_QUANTISE_X = 2
+LAG_LAYER1 = 3
+LAG_ACTIVATE1 = 4
+LAG_GATE = 5
+LAG_TRANSPOSE_H = 6
+LAG_COPY_H = 7
+LAG_QUANTISE_H = 8
+LAG_LAYER2 = (SLICES - 1) + LAG_QUANTISE_H + 1
+LAG_BIAS2 = LAG_LAYER2 + 1
+LAG_SILU2 = LAG_LAYER2 + 2
+LAG_SUM = LAG_LAYER2 + 3
+STEPS = UNITS + LAG_SUM
+SPREAD_B2_FROM = (SLICES - 1) + LAG_ACTIVATE1
+SPREAD_B2_PER_STEP = 2
+
+FLOPS = 2 * (2 * EDGES) * D * H * 2
+
+
+def is_unit(unit):
+    return 0 <= unit < UNITS
+
+
+def starts_x_run(unit):
+    return is_unit(unit) and unit % X_RUN == 0
+
+
+def ends_round(unit):
+    return is_unit(unit) and unit % SLICES == SLICES - 1
+
+
+def tile_node_interaction_kernel(
+    tc, node_embed, x_edge_c, ori, W1_words, W1_scales, b1, W2_words, W2_scales, b2, edge_num, out
+):
+    nc = tc.nc
+    assert edge_num == EDGES
+    x_halves = (node_embed, ori)
+    out_rows = out.rearrange("e c d -> e (c d)")
+
+    with ExitStack() as stack:
+        stack.enter_context(tc.manual_schedule())
+        keep = stack.enter_context(tc.tile_pool(name="keep", bufs=1))
+        x_pool = stack.enter_context(tc.tile_pool(name="x_pool", bufs=2))
+        stream = stack.enter_context(tc.tile_pool(name="stream", bufs=3))
+        per_round = stack.enter_context(tc.tile_pool(name="per_round", bufs=2))
+        psum_t = stack.enter_context(tc.psum_pool(name="psum_t", bufs=2))
+        psum_1 = stack.enter_context(tc.psum_pool(name="psum_1", bufs=1))
+        psum_2 = stack.enter_context(tc.psum_pool(name="psum_2", bufs=4))
+
+        ident_f32 = keep.tile([P, P], F32)
+        ident_bf16 = keep.tile([P, P], BF16)
+        w1_words = keep.tile([P, SLICES, PACK * H], U8, align_bytes=64)
+        w1_scales = keep.tile([P, SLICES, H], U8, align_bytes=64)
+        w2_words = keep.tile([P, PACK * D], U8, align_bytes=64)
+        w2_scales = keep.tile([P, D], U8, align_bytes=64)
+        gate_rows = keep.tile([P, ROUNDS, H], BF16)
+        bias_rows = keep.tile([P, N_TILE], BF16)
+        bias_all = keep.tile([P, BIAS_ROWS, N_TILE], F32)
+
+        x_tiles, xt_banks, x_grouped, x_codes, x_scales = {}, {}, {}, {}, {}
+        sums1, activated, h_sorted, ht_banks, h_grouped, h_codes, h_scales = {}, {}, {}, {}, {}, {}, {}
+        y_banks, y_biased, y_activated = {}, {}, {}
+
+        def new_x_tile(rnd):
+            x_tile = x_pool.tile([P, 2, D], BF16)
+            x_tiles[rnd] = x_tile
+
+        def load_x_chunk(rnd, chunk):
+            rows = slice(rnd * P, (rnd + 1) * P)
+            cols = slice(chunk * X_CHUNK, (chunk + 1) * X_CHUNK)
+            for half in range(2):
+                nc.sync.dma_start(out=x_tiles[rnd][:, half, cols], in_=x_halves[half][rows, cols])
+
+        def load_x(rnd):
+            new_x_tile(rnd)
+            for chunk in range(X_CHUNKS):
+                load_x_chunk(rnd, chunk)
+
+        def load_scale_rows(plane, scale_rows):
+            for quadrant in range(4):
+                nc.sync.dma_start(
+                    out=plane[32 * quadrant : 32 * quadrant + 4].bitcast(I32),
+                    in_=scale_rows[4 * quadrant : 4 * quadrant + 4].bitcast(I32),
+                )
+
+        nc.vector.memset(bias_rows[:], 0.0)
+        nc.vector.memset(w1_scales[:].bitcast(I32), 0)
+        nc.vector.memset(w2_scales[:].bitcast(I32), 0)
+        make_identity(nc, ident_f32[:])
+        make_identity(nc, ident_bf16[:])
+
+        new_x_tile(0)
+        load_x_chunk(0, 0)
+        nc.sync.dma_start(out=bias_rows[0:SLICES, :], in_=b2.rearrange("(c n) -> c n", n=N_TILE))
+        nc.sync.dma_start(out=bias_rows[B1_ROW : B1_ROW + 1, :], in_=b1.rearrange("(o n) -> o n", o=1))
+        load_scale_rows(w1_scales, W1_scales.rearrange("g q n -> q g n"))
+        chunks_loaded = 1
+        for g in range(SLICES):
+            while chunks_loaded * X_CHUNK < (g + 1) * K_PASS:
+                load_x_chunk(0, chunks_loaded)
+                chunks_loaded += 1
+            nc.sync.dma_start(
+                out=w1_words[:, g, :].bitcast(I32),
+                in_=W1_words[g].rearrange("p n t -> p (n t)").bitcast(I32),
+            )
+        nc.sync.dma_start(out=gate_rows[:], in_=x_edge_c.rearrange("(i p) h -> p i h", p=P))
+        load_x(1)
+        load_scale_rows(w2_scales, W2_scales[0])
+        w2_bytes = W2_words[0].rearrange("p n t -> p (n t)")
+        for c in range(SLICES):
+            byte_cols = slice(c * PACK * N_TILE, (c + 1) * PACK * N_TILE)
+            nc.sync.dma_start(out=w2_words[:, byte_cols].bitcast(I32), in_=w2_bytes[:, byte_cols].bitcast(I32))
+
+        def spread_bias(row):
+            spread = psum_2.tile([P, N_TILE], F32, tag="y")
+            nc.tensor.matmul(
+                out=spread[:],
+                lhsT=ident_bf16[:, row : row + 1].to_broadcast([P, P]),
+                rhs=bias_rows[:],
+                start=True,
+                stop=True,
+            )
+            nc.vector.tensor_copy(out=bias_all[:, row, :], in_=spread[:])
+
+        def transpose_x(unit):
+            rnd, g = divmod(unit, SLICES)
+            xt_bank = psum_t.tile([P, 2, 2, P], F32)
+            for half in range(2):
+                words = x_tiles[rnd][:, half, :].bitcast(F32)
+                for u in range(2):
+                    nc.tensor.transpose(
+                        out=xt_bank[:, half, u, :],
+                        in_=words[:, g * 2 * P + u : (g + 1) * 2 * P : 2],
+                        identity=ident_f32[:],
+                    )
+            xt_banks[unit] = xt_bank
+
+        def copy_x_run(first_unit):
+            grouped = stream.tile([P, X_RUN, 2, P, PACK], BF16, align_bytes=64, tag="x_grouped")
+            for j in range(X_RUN):
+                nc.scalar.copy(
+                    out=grouped[:, j].bitcast(F32),
+                    in_=xt_banks[first_unit + j][:].rearrange("p a u r -> p a r u"),
+                )
+            x_grouped[first_unit] = grouped
+
+        def quantise_x_run(first_unit):
+            codes = stream.tile([P, X_RUN, 2 * P], U32, align_bytes=64, tag="x_codes")
+            scales = stream.tile([P, X_RUN, 2 * P], U8, align_bytes=64, tag="x_scales")
+            nc.vector.quantize_mx(
+                out=codes[:].rearrange("p j r -> p (j r)").bitcast(FP8X4),
+                scales=scales[:].rearrange("p j r -> p (j r)"),
+                in_=x_grouped[first_unit][:].rearrange("p j a r t -> p (j a r t)"),
+            )
+            for j in range(X_RUN):
+                x_codes[first_unit + j], x_scales[first_unit + j] = codes[:, j, :], scales[:, j, :]
+
+        def layer1(unit):
+            rnd, g = divmod(unit, SLICES)
+            if g == 0:
+                sums1[rnd] = [psum_1.tile([P, H], F32, name="sum1_half%d" % half) for half in range(2)]
+            for half in range(2):
+                rows = slice(half * P, (half + 1) * P)
+                nc.tensor.matmul_mx(
+                    out=sums1[rnd][half][:],
+                    lhsT=x_codes[unit][:, rows].bitcast(FP8X4),
+                    lhsT_scale=x_scales[unit][:, rows],
+                    rhs=w1_words[:, g, :].bitcast(FP8X4),
+                    rhs_scale=w1_scales[:, g, :],
+                    start=(g == 0),
+                    stop=(g == SLICES - 1),
+                )
+
+        def activate1(rnd):
+            biased = per_round.tile([P, 2, H], F32, tag="biased1")
+            for half in range(2):
+                nc.vector.tensor_tensor(
+                    out=biased[:, half, :], in0=sums1[rnd][half][:], in1=bias_all[:, B1_ROW, :], op=ADD
+                )
+            silu1 = per_round.tile([P, 2, H], F32, tag="silu1")
+            nc.scalar.activation(out=silu1[:], in_=biased[:], func=SILU)
+            activated[rnd] = silu1
+
+        def gate(rnd):
+            h_tile = per_round.tile([P, 2, PACK, P], BF16, tag="h_sorted")
+            for half in range(2):
+                nc.vector.tensor_tensor(
+                    out=h_tile[:, half],
+                    in0=activated[rnd][:, half, :].rearrange("r (p t) -> r t p", t=PACK),
+                    in1=gate_rows[:, rnd, :].rearrange("r (p t) -> r t p", t=PACK),
+                    op=MULT,
+                )
+            h_sorted[rnd] = h_tile
+
+        def transpose_h(rnd):
+            ht_bank = psum_2.tile([P, 2, PACK, P], BF16, tag="y")
+            for half in range(2):
+                for t in range(PACK):
+                    nc.tensor.transpose(
+                        out=ht_bank[:, half, t, :], in_=h_sorted[rnd][:, half, t, :], identity=ident_bf16[:]
+                    )
+            ht_banks[rnd] = ht_bank
+
+        def copy_h(rnd):
+            grouped = per_round.tile([P, 2, P, PACK], BF16, align_bytes=64, tag="h_grouped")
+            nc.scalar.copy(out=grouped[:], in_=ht_banks[rnd][:].rearrange("p a t r -> p a r t"))
+            h_grouped[rnd] = grouped
+
+        def quantise_h(rnd):
+            codes = per_round.tile([P, 2 * P], U32, align_bytes=64, tag="h_codes")
+            scales = per_round.tile([P, 2 * P], U8, align_bytes=64, tag="h_scales")
+            nc.vector.quantize_mx(
+                out=codes[:].bitcast(FP8X4),
+                scales=scales[:],
+                in_=h_grouped[rnd][:].rearrange("p a r t -> p (a r t)"),
+            )
+            h_codes[rnd], h_scales[rnd] = codes, scales
+
+        def layer2(unit):
+            rnd, c = divmod(unit, SLICES)
+            y_banks[unit] = [psum_2.tile([P, N_TILE], F32, name="y_half%d" % half, tag="y") for half in range(2)]
+            for half in range(2):
+                rows = slice(half * P, (half + 1) * P)
+                nc.tensor.matmul_mx(
+                    out=y_banks[unit][half][:],
+                    lhsT=h_codes[rnd][:, rows].bitcast(FP8X4),
+                    lhsT_scale=h_scales[rnd][:, rows],
+                    rhs=w2_words[:, c * PACK * N_TILE : (c + 1) * PACK * N_TILE].bitcast(FP8X4),
+                    rhs_scale=w2_scales[:, c * N_TILE : (c + 1) * N_TILE],
+                    start=True,
+                    stop=True,
+                )
+
+        def bias2(unit):
+            c = unit % SLICES
+            biased = stream.tile([P, 2, N_TILE], F32, tag="biased2")
+            for half in range(2):
+                nc.vector.tensor_tensor(
+                    out=biased[:, half, :], in0=y_banks[unit][half][:], in1=bias_all[:, c, :], op=ADD
+                )
+            y_biased[unit] = biased
+
+        def silu2(unit):
+            silu = stream.tile([P, 2, N_TILE], F32, tag="silu2")
+            nc.scalar.activation(out=silu[:], in_=y_biased[unit][:], func=SILU)
+            y_activated[unit] = silu
+
+        def sum_and_store(unit):
+            rnd, c = divmod(unit, SLICES)
+            total = stream.tile([P, N_TILE], F32, tag="total")
+            nc.gpsimd.tensor_tensor(
+                out=total[:], in0=y_activated[unit][:, 0, :], in1=y_activated[unit][:, 1, :], op=ADD
+            )
+            nc.sync.dma_start(
+                out=out_rows[rnd * P : (rnd + 1) * P, c * N_TILE : (c + 1) * N_TILE], in_=total[:]
+            )
+
+        for step in range(STEPS):
+            if is_unit(step - LAG_SUM):
+                sum_and_store(step - LAG_SUM)
+            if is_unit(step - LAG_SILU2):
+                silu2(step - LAG_SILU2)
+            if is_unit(step - LAG_BIAS2):
+                bias2(step - LAG_BIAS2)
+            if is_unit(step - LAG_LAYER2):
+                layer2(step - LAG_LAYER2)
+            if ends_round(step - LAG_QUANTISE_H):
+                quantise_h((step - LAG_QUANTISE_H) // SLICES)
+            if ends_round(step - LAG_COPY_H):
+                copy_h((step - LAG_COPY_H) // SLICES)
+            if ends_round(step - LAG_TRANSPOSE_H):
+                transpose_h((step - LAG_TRANSPOSE_H) // SLICES)
+            if ends_round(step - LAG_GATE):
+                gate((step - LAG_GATE) // SLICES)
+            if ends_round(step - LAG_ACTIVATE1):
+                activate1((step - LAG_ACTIVATE1) // SLICES)
+            if is_unit(step - LAG_LAYER1):
+                layer1(step - LAG_LAYER1)
+            if starts_x_run(step - LAG_QUANTISE_X):
+                quantise_x_run(step - LAG_QUANTISE_X)
+            if starts_x_run(step - LAG_COPY_X):
+                copy_x_run(step - LAG_COPY_X)
+            if starts_x_run(step):
+                for unit in range(step, step + X_RUN):
+                    transpose_x(unit)
+                    if ends_round(unit) and unit // SLICES + 2 < ROUNDS:
+                        load_x(unit // SLICES + 2)
+            if step == 0:
+                spread_bias(B1_ROW)
+            for row in range(SLICES):
+                if row // SPREAD_B2_PER_STEP == step - SPREAD_B2_FROM:
+                    spread_bias(row)

@@ -28,20 +28,24 @@ B1_ROW = SLICES
 BIAS_ROWS = SLICES + 1
 
 LAG_COPY_X = 1
-LAG_QUANTISE_X = 2
-LAG_LAYER1 = 3
-LAG_ACTIVATE1 = 4
-LAG_GATE = 5
-LAG_TRANSPOSE_H = 6
-LAG_COPY_H = 7
-LAG_QUANTISE_H = 8
+LAG_QUANTISE_X = 3
+LAG_LAYER1 = 4
+LAG_ACTIVATE1 = 5
+LAG_GATE = 6
+LAG_TRANSPOSE_H = 7
+LAG_COPY_H = 8
+LAG_QUANTISE_H = 9
 LAG_LAYER2 = (SLICES - 1) + LAG_QUANTISE_H + 1
 LAG_BIAS2 = LAG_LAYER2 + 1
 LAG_SILU2 = LAG_LAYER2 + 2
 LAG_SUM = LAG_LAYER2 + 3
 STEPS = UNITS + LAG_SUM
-SPREAD_B2_FROM = (SLICES - 1) + LAG_ACTIVATE1
-SPREAD_B2_PER_STEP = 2
+X_AHEAD = LAG_LAYER1 + X_RUN
+BIASED_BUFS = 3
+SILU_BUFS = 4
+TOTAL_BUFS = 6
+SPREAD_FROM = 0
+SPREAD_PER_STEP = 3
 
 FLOPS = 2 * (2 * EDGES) * D * H * 2
 
@@ -119,21 +123,24 @@ def tile_node_interaction_kernel(
         make_identity(nc, ident_bf16[:])
 
         new_x_tile(0)
+        new_x_tile(1)
         load_x_chunk(0, 0)
         nc.sync.dma_start(out=bias_rows[0:SLICES, :], in_=b2.rearrange("(c n) -> c n", n=N_TILE))
         nc.sync.dma_start(out=bias_rows[B1_ROW : B1_ROW + 1, :], in_=b1.rearrange("(o n) -> o n", o=1))
         load_scale_rows(w1_scales, W1_scales.rearrange("g q n -> q g n"))
         chunks_loaded = 1
         for g in range(SLICES):
-            while chunks_loaded * X_CHUNK < (g + 1) * K_PASS:
-                load_x_chunk(0, chunks_loaded)
+            while chunks_loaded * X_CHUNK < (g + X_AHEAD) * K_PASS:
+                load_x_chunk(chunks_loaded // X_CHUNKS, chunks_loaded % X_CHUNKS)
                 chunks_loaded += 1
             nc.sync.dma_start(
                 out=w1_words[:, g, :].bitcast(I32),
                 in_=W1_words[g].rearrange("p n t -> p (n t)").bitcast(I32),
             )
         nc.sync.dma_start(out=gate_rows[:], in_=x_edge_c.rearrange("(i p) h -> p i h", p=P))
-        load_x(1)
+        while chunks_loaded < 2 * X_CHUNKS:
+            load_x_chunk(chunks_loaded // X_CHUNKS, chunks_loaded % X_CHUNKS)
+            chunks_loaded += 1
         load_scale_rows(w2_scales, W2_scales[0])
         w2_bytes = W2_words[0].rearrange("p n t -> p (n t)")
         for c in range(SLICES):
@@ -262,7 +269,7 @@ def tile_node_interaction_kernel(
 
         def bias2(unit):
             c = unit % SLICES
-            biased = stream.tile([P, 2, N_TILE], F32, tag="biased2")
+            biased = stream.tile([P, 2, N_TILE], F32, tag="biased2", bufs=BIASED_BUFS)
             for half in range(2):
                 nc.vector.tensor_tensor(
                     out=biased[:, half, :], in0=y_banks[unit][half][:], in1=bias_all[:, c, :], op=ADD
@@ -270,13 +277,13 @@ def tile_node_interaction_kernel(
             y_biased[unit] = biased
 
         def silu2(unit):
-            silu = stream.tile([P, 2, N_TILE], F32, tag="silu2")
+            silu = stream.tile([P, 2, N_TILE], F32, tag="silu2", bufs=SILU_BUFS)
             nc.scalar.activation(out=silu[:], in_=y_biased[unit][:], func=SILU)
             y_activated[unit] = silu
 
         def sum_and_store(unit):
             rnd, c = divmod(unit, SLICES)
-            total = stream.tile([P, N_TILE], F32, tag="total")
+            total = stream.tile([P, N_TILE], F32, tag="total", bufs=TOTAL_BUFS)
             nc.gpsimd.tensor_tensor(
                 out=total[:], in0=y_activated[unit][:, 0, :], in1=y_activated[unit][:, 1, :], op=ADD
             )
@@ -314,8 +321,6 @@ def tile_node_interaction_kernel(
                     transpose_x(unit)
                     if ends_round(unit) and unit // SLICES + 2 < ROUNDS:
                         load_x(unit // SLICES + 2)
-            if step == 0:
-                spread_bias(B1_ROW)
-            for row in range(SLICES):
-                if row // SPREAD_B2_PER_STEP == step - SPREAD_B2_FROM:
+            for row in range(BIAS_ROWS):
+                if row // SPREAD_PER_STEP == step - SPREAD_FROM:
                     spread_bias(row)

@@ -24,8 +24,15 @@ UNITS = ROUNDS * SLICES
 X_CHUNKS = 4
 X_CHUNK = D // X_CHUNKS
 X_RUN = 2
-B1_ROW = SLICES
-BIAS_ROWS = SLICES + 1
+BLOCK = 32
+BLOCKS = P // BLOCK
+C_TILES = D // P
+C_BLOCK = D // BLOCKS
+UNIT_TILES = N_TILE // P
+W2_CHUNKS = 4
+CHUNK_TILES = C_TILES // W2_CHUNKS
+STORE_ORDER = (0, 2, 1, 3)
+GROUP_UNITS = 2
 
 LAG_COPY_X = 1
 LAG_QUANTISE_X = 3
@@ -36,16 +43,15 @@ LAG_TRANSPOSE_H = 7
 LAG_COPY_H = 8
 LAG_QUANTISE_H = 9
 LAG_LAYER2 = (SLICES - 1) + LAG_QUANTISE_H + 1
-LAG_BIAS2 = LAG_LAYER2 + 1
-LAG_SILU2 = LAG_LAYER2 + 2
-LAG_SUM = LAG_LAYER2 + 3
-STEPS = UNITS + LAG_SUM
+LAG_SILU2 = LAG_LAYER2 + 1
+LAG_SUM = LAG_LAYER2 + 2
+LAG_STORE = LAG_LAYER2 + 3
+STEPS = UNITS + LAG_STORE
+SORT_W2_FROM = LAG_LAYER2 - 2
 X_AHEAD = LAG_LAYER1 + X_RUN
-BIASED_BUFS = 3
 SILU_BUFS = 4
-TOTAL_BUFS = 6
-SPREAD_FROM = 0
-SPREAD_PER_STEP = 3
+TOTAL_BUFS = 2
+TURNED_BUFS = 3
 
 FLOPS = 2 * (2 * EDGES) * D * H * 2
 
@@ -62,6 +68,10 @@ def ends_round(unit):
     return is_unit(unit) and unit % SLICES == SLICES - 1
 
 
+def ends_group(unit):
+    return is_unit(unit) and (unit % SLICES % GROUP_UNITS == GROUP_UNITS - 1 or ends_round(unit))
+
+
 def tile_node_interaction_kernel(
     tc, node_embed, x_edge_c, ori, W1_words, W1_scales, b1, W2_words, W2_scales, b2, edge_num, out
 ):
@@ -74,6 +84,7 @@ def tile_node_interaction_kernel(
         stack.enter_context(tc.manual_schedule())
         keep = stack.enter_context(tc.tile_pool(name="keep", bufs=1))
         x_pool = stack.enter_context(tc.tile_pool(name="x_pool", bufs=2))
+        w2_stage = stack.enter_context(tc.tile_pool(name="w2_stage", bufs=W2_CHUNKS))
         stream = stack.enter_context(tc.tile_pool(name="stream", bufs=3))
         per_round = stack.enter_context(tc.tile_pool(name="per_round", bufs=2))
         psum_t = stack.enter_context(tc.psum_pool(name="psum_t", bufs=2))
@@ -84,15 +95,18 @@ def tile_node_interaction_kernel(
         ident_bf16 = keep.tile([P, P], BF16)
         w1_words = keep.tile([P, SLICES, PACK * H], U8, align_bytes=64)
         w1_scales = keep.tile([P, SLICES, H], U8, align_bytes=64)
-        w2_words = keep.tile([P, PACK * D], U8, align_bytes=64)
-        w2_scales = keep.tile([P, D], U8, align_bytes=64)
+        w2_words = keep.tile([P, C_TILES, BLOCKS, BLOCK], I32, align_bytes=64)
+        w2_scale_rows = keep.tile([P, D], U8, align_bytes=64)
+        w2_scales = keep.tile([P, C_TILES, BLOCKS, BLOCK // 4], I32, align_bytes=64)
         gate_rows = keep.tile([P, ROUNDS, H], BF16)
-        bias_rows = keep.tile([P, N_TILE], BF16)
-        bias_all = keep.tile([P, BIAS_ROWS, N_TILE], F32)
+        b1_row = keep.tile([P, H], BF16)
+        b1_all = keep.tile([P, H], F32)
+        b2_rows = keep.tile([P, P], BF16)
+        b2_cols = keep.tile([P, C_TILES], F32)
 
         x_tiles, xt_banks, x_grouped, x_codes, x_scales = {}, {}, {}, {}, {}
         sums1, activated, h_sorted, ht_banks, h_grouped, h_codes, h_scales = {}, {}, {}, {}, {}, {}, {}
-        y_banks, y_biased, y_activated = {}, {}, {}
+        w2_raw, y_banks, y_activated, totals = {}, {}, {}, {}
 
         def new_x_tile(rnd):
             x_tile = x_pool.tile([P, 2, D], BF16)
@@ -116,18 +130,22 @@ def tile_node_interaction_kernel(
                     in_=scale_rows[4 * quadrant : 4 * quadrant + 4].bitcast(I32),
                 )
 
-        nc.vector.memset(bias_rows[:], 0.0)
         nc.vector.memset(w1_scales[:].bitcast(I32), 0)
-        nc.vector.memset(w2_scales[:].bitcast(I32), 0)
+        nc.vector.memset(b1_row[:], 0.0)
+        nc.vector.memset(b2_rows[:], 0.0)
+        nc.vector.memset(w2_scale_rows[:].bitcast(I32), 0)
         make_identity(nc, ident_f32[:])
         make_identity(nc, ident_bf16[:])
 
         new_x_tile(0)
         new_x_tile(1)
         load_x_chunk(0, 0)
-        nc.sync.dma_start(out=bias_rows[0:SLICES, :], in_=b2.rearrange("(c n) -> c n", n=N_TILE))
-        nc.sync.dma_start(out=bias_rows[B1_ROW : B1_ROW + 1, :], in_=b1.rearrange("(o n) -> o n", o=1))
         load_scale_rows(w1_scales, W1_scales.rearrange("g q n -> q g n"))
+        nc.sync.dma_start(out=b1_row[0:1, :], in_=b1.rearrange("(o n) -> o n", o=1))
+        nc.sync.dma_start(
+            out=b2_rows[0:C_TILES, :].rearrange("c (a j) -> c a j", a=BLOCKS),
+            in_=b2.rearrange("(a c j) -> c a j", a=BLOCKS, j=BLOCK),
+        )
         chunks_loaded = 1
         for g in range(SLICES):
             while chunks_loaded * X_CHUNK < (g + X_AHEAD) * K_PASS:
@@ -141,22 +159,41 @@ def tile_node_interaction_kernel(
         while chunks_loaded < 2 * X_CHUNKS:
             load_x_chunk(chunks_loaded // X_CHUNKS, chunks_loaded % X_CHUNKS)
             chunks_loaded += 1
-        load_scale_rows(w2_scales, W2_scales[0])
-        w2_bytes = W2_words[0].rearrange("p n t -> p (n t)")
-        for c in range(SLICES):
-            byte_cols = slice(c * PACK * N_TILE, (c + 1) * PACK * N_TILE)
-            nc.sync.dma_start(out=w2_words[:, byte_cols].bitcast(I32), in_=w2_bytes[:, byte_cols].bitcast(I32))
+        load_scale_rows(w2_scale_rows, W2_scales[0])
+        w2_blocks = W2_words[0].rearrange("p n t -> p (n t)").bitcast(I32).rearrange("p (a m) -> p a m", a=BLOCKS)
+        for chunk in range(W2_CHUNKS):
+            raw = w2_stage.tile([P, BLOCKS, CHUNK_TILES * BLOCK], I32)
+            m_cols = slice(chunk * CHUNK_TILES * BLOCK, (chunk + 1) * CHUNK_TILES * BLOCK)
+            nc.sync.dma_start(out=raw[:], in_=w2_blocks[:, :, m_cols])
+            w2_raw[chunk] = raw
 
-        def spread_bias(row):
-            spread = psum_2.tile([P, N_TILE], F32, tag="y")
+        def spread_b1():
+            spread = psum_2.tile([P, H], F32, tag="y")
             nc.tensor.matmul(
                 out=spread[:],
-                lhsT=ident_bf16[:, row : row + 1].to_broadcast([P, P]),
-                rhs=bias_rows[:],
+                lhsT=ident_bf16[:, 0:1].to_broadcast([P, P]),
+                rhs=b1_row[:],
                 start=True,
                 stop=True,
             )
-            nc.vector.tensor_copy(out=bias_all[:, row, :], in_=spread[:])
+            nc.vector.tensor_copy(out=b1_all[:], in_=spread[:])
+
+        def turn_b2():
+            turned = psum_2.tile([P, P], BF16, tag="y")
+            nc.tensor.transpose(out=turned[:], in_=b2_rows[:], identity=ident_bf16[:])
+            nc.vector.tensor_copy(out=b2_cols[:], in_=turned[:, 0:C_TILES])
+
+        def sort_w2_scales():
+            nc.vector.tensor_copy(
+                out=w2_scales[:],
+                in_=w2_scale_rows[:].bitcast(I32).rearrange("p (a c j) -> p c a j", a=BLOCKS, c=C_TILES),
+            )
+
+        def sort_w2(chunk):
+            nc.vector.tensor_copy(
+                out=w2_words[:, chunk * CHUNK_TILES : (chunk + 1) * CHUNK_TILES],
+                in_=w2_raw[chunk][:].rearrange("p a (c j) -> p c a j", j=BLOCK),
+            )
 
         def transpose_x(unit):
             rnd, g = divmod(unit, SLICES)
@@ -171,10 +208,10 @@ def tile_node_interaction_kernel(
                     )
             xt_banks[unit] = xt_bank
 
-        def copy_x_run(first_unit):
+        def copy_x_run(first_unit, copy):
             grouped = stream.tile([P, X_RUN, 2, P, PACK], BF16, align_bytes=64, tag="x_grouped")
             for j in range(X_RUN):
-                nc.scalar.copy(
+                copy(
                     out=grouped[:, j].bitcast(F32),
                     in_=xt_banks[first_unit + j][:].rearrange("p a u r -> p a r u"),
                 )
@@ -211,7 +248,7 @@ def tile_node_interaction_kernel(
             biased = per_round.tile([P, 2, H], F32, tag="biased1")
             for half in range(2):
                 nc.vector.tensor_tensor(
-                    out=biased[:, half, :], in0=sums1[rnd][half][:], in1=bias_all[:, B1_ROW, :], op=ADD
+                    out=biased[:, half, :], in0=sums1[rnd][half][:], in1=b1_all[:], op=ADD
                 )
             silu1 = per_round.tile([P, 2, H], F32, tag="silu1")
             nc.scalar.activation(out=silu1[:], in_=biased[:], func=SILU)
@@ -254,50 +291,73 @@ def tile_node_interaction_kernel(
 
         def layer2(unit):
             rnd, c = divmod(unit, SLICES)
-            y_banks[unit] = [psum_2.tile([P, N_TILE], F32, name="y_half%d" % half, tag="y") for half in range(2)]
-            for half in range(2):
-                rows = slice(half * P, (half + 1) * P)
+            y_banks[unit] = [
+                psum_2.tile([P, 2, 2 * P], F32, name="y_pair%d" % pair, tag="y") for pair in range(UNIT_TILES // 2)
+            ]
+            for tile in range(UNIT_TILES):
+                c_tile = c * UNIT_TILES + tile
                 nc.tensor.matmul_mx(
-                    out=y_banks[unit][half][:],
-                    lhsT=h_codes[rnd][:, rows].bitcast(FP8X4),
-                    lhsT_scale=h_scales[rnd][:, rows],
-                    rhs=w2_words[:, c * PACK * N_TILE : (c + 1) * PACK * N_TILE].bitcast(FP8X4),
-                    rhs_scale=w2_scales[:, c * N_TILE : (c + 1) * N_TILE],
+                    out=y_banks[unit][tile // 2][:, tile % 2, :],
+                    lhsT=w2_words[:, c_tile].rearrange("p a j -> p (a j)").bitcast(FP8X4),
+                    lhsT_scale=w2_scales[:, c_tile].rearrange("p a j -> p (a j)").bitcast(U8),
+                    rhs=h_codes[rnd][:].bitcast(FP8X4),
+                    rhs_scale=h_scales[rnd][:],
                     start=True,
                     stop=True,
                 )
 
-        def bias2(unit):
-            c = unit % SLICES
-            biased = stream.tile([P, 2, N_TILE], F32, tag="biased2", bufs=BIASED_BUFS)
-            for half in range(2):
-                nc.vector.tensor_tensor(
-                    out=biased[:, half, :], in0=y_banks[unit][half][:], in1=bias_all[:, c, :], op=ADD
-                )
-            y_biased[unit] = biased
-
         def silu2(unit):
-            silu = stream.tile([P, 2, N_TILE], F32, tag="silu2", bufs=SILU_BUFS)
-            nc.scalar.activation(out=silu[:], in_=y_biased[unit][:], func=SILU)
+            c = unit % SLICES
+            silu = stream.tile([P, UNIT_TILES, 2, P], F32, tag="silu2", bufs=SILU_BUFS)
+            for tile in range(UNIT_TILES):
+                c_tile = c * UNIT_TILES + tile
+                nc.scalar.activation(
+                    out=silu[:, tile].rearrange("p a r -> p (a r)"),
+                    in_=y_banks[unit][tile // 2][:, tile % 2, :],
+                    func=SILU,
+                    bias=b2_cols[:, c_tile : c_tile + 1],
+                )
             y_activated[unit] = silu
 
-        def sum_and_store(unit):
-            rnd, c = divmod(unit, SLICES)
-            total = stream.tile([P, N_TILE], F32, tag="total", bufs=TOTAL_BUFS)
+        def add_halves(unit):
+            c = unit % SLICES
+            first = unit - c % GROUP_UNITS
+            if unit == first:
+                units = min(GROUP_UNITS, SLICES - c)
+                total = stream.tile([P, BLOCKS, units * UNIT_TILES, BLOCK], F32, align_bytes=64, tag="total", bufs=TOTAL_BUFS)
+                totals[first] = total
+            tiles = slice((unit - first) * UNIT_TILES, (unit - first + 1) * UNIT_TILES)
             nc.gpsimd.tensor_tensor(
-                out=total[:], in0=y_activated[unit][:, 0, :], in1=y_activated[unit][:, 1, :], op=ADD
-            )
-            nc.sync.dma_start(
-                out=out_rows[rnd * P : (rnd + 1) * P, c * N_TILE : (c + 1) * N_TILE], in_=total[:]
+                out=totals[first][:, :, tiles, :].rearrange("p b c i -> p c b i"),
+                in0=y_activated[unit][:, :, 0, :].rearrange("p c (b i) -> p c b i", b=BLOCKS),
+                in1=y_activated[unit][:, :, 1, :].rearrange("p c (b i) -> p c b i", b=BLOCKS),
+                op=ADD,
             )
 
+        def turn_and_store(last_unit):
+            rnd, c = divmod(last_unit, SLICES)
+            first = last_unit - c % GROUP_UNITS
+            tiles = (last_unit - first + 1) * UNIT_TILES
+            turned = stream.tile([P, BLOCKS, tiles, BLOCK], F32, align_bytes=64, tag="turned", bufs=TURNED_BUFS)
+            nc.vector.transpose(
+                out=turned[:].rearrange("p b c j -> p (b c j)"),
+                in_=totals[first][:].rearrange("p b c i -> p (b c i)"),
+            )
+            first_col = first % SLICES * UNIT_TILES * BLOCK
+            for a in STORE_ORDER:
+                cols = slice(a * C_BLOCK + first_col, a * C_BLOCK + first_col + tiles * BLOCK)
+                nc.sync.dma_start(
+                    out=out_rows[rnd * P : (rnd + 1) * P, cols].rearrange("(b i) n -> i b n", i=BLOCK),
+                    in_=turned[a * BLOCK : (a + 1) * BLOCK].rearrange("p b c j -> p b (c j)"),
+                )
+
         for step in range(STEPS):
+            if ends_group(step - LAG_STORE):
+                turn_and_store(step - LAG_STORE)
             if is_unit(step - LAG_SUM):
-                sum_and_store(step - LAG_SUM)
+                add_halves(step - LAG_SUM)
             if is_unit(step - LAG_SILU2):
                 silu2(step - LAG_SILU2)
-            if is_unit(step - LAG_BIAS2):
-                bias2(step - LAG_BIAS2)
             if is_unit(step - LAG_LAYER2):
                 layer2(step - LAG_LAYER2)
             if ends_round(step - LAG_QUANTISE_H):
@@ -315,12 +375,17 @@ def tile_node_interaction_kernel(
             if starts_x_run(step - LAG_QUANTISE_X):
                 quantise_x_run(step - LAG_QUANTISE_X)
             if starts_x_run(step - LAG_COPY_X):
-                copy_x_run(step - LAG_COPY_X)
+                copy_x_run(step - LAG_COPY_X, nc.scalar.copy if step < LAG_LAYER2 else nc.vector.tensor_copy)
             if starts_x_run(step):
                 for unit in range(step, step + X_RUN):
                     transpose_x(unit)
                     if ends_round(unit) and unit // SLICES + 2 < ROUNDS:
                         load_x(unit // SLICES + 2)
-            for row in range(BIAS_ROWS):
-                if row // SPREAD_PER_STEP == step - SPREAD_FROM:
-                    spread_bias(row)
+            if step == 1:
+                spread_b1()
+                turn_b2()
+            if step == SORT_W2_FROM:
+                sort_w2_scales()
+            for chunk in range(W2_CHUNKS):
+                if step == SORT_W2_FROM + 2 * chunk:
+                    sort_w2(chunk)

@@ -21,9 +21,9 @@ N_TILE = 512
 ROUNDS = EDGES // P
 SLICES = D // K_PASS
 UNITS = ROUNDS * SLICES
-X_CHUNKS = 4
-X_CHUNK = D // X_CHUNKS
+X_CHUNK_UNITS = 4
 X_RUN = 2
+SCALAR_COPIES = ()
 BLOCK = 32
 BLOCKS = P // BLOCK
 C_TILES = D // P
@@ -35,20 +35,23 @@ STORE_ORDER = (0, 2, 1, 3)
 GROUP_UNITS = 2
 
 LAG_COPY_X = 1
-LAG_QUANTISE_X = 3
-LAG_LAYER1 = 4
-LAG_ACTIVATE1 = 5
-LAG_GATE = 6
-LAG_TRANSPOSE_H = 7
-LAG_COPY_H = 8
-LAG_QUANTISE_H = 9
+LAG_QUANTISE_X = 2
+LAG_LAYER1 = 3
+LAG_ACTIVATE1 = LAG_LAYER1 + 1
+LAG_GATE = LAG_LAYER1 + 1
+LAG_TRANSPOSE_H = LAG_LAYER1 + 2
+LAG_COPY_H = LAG_LAYER1 + 2
+LAG_QUANTISE_H = LAG_LAYER1 + 2
 LAG_LAYER2 = (SLICES - 1) + LAG_QUANTISE_H + 1
-LAG_SILU2 = LAG_LAYER2 + 1
-LAG_SUM = LAG_LAYER2 + 2
-LAG_STORE = LAG_LAYER2 + 3
-STEPS = UNITS + LAG_STORE
+LAG_SILU2 = 1
+LAG_SUM = 2
+LAG_STORE = 3
+GAP = 0
+X_SLOTS = list(range(SLICES)) + [None] * GAP + list(range(SLICES, UNITS))
+Y_SLOTS = [None] * LAG_LAYER2 + list(range(SLICES)) + [None] * GAP + list(range(SLICES, UNITS))
+STEPS = len(Y_SLOTS) + LAG_STORE
 SORT_W2_FROM = LAG_LAYER2 - 2
-X_AHEAD = LAG_LAYER1 + X_RUN
+X_LEAD = 4
 SILU_BUFS = 4
 TOTAL_BUFS = 2
 TURNED_BUFS = 3
@@ -56,20 +59,16 @@ TURNED_BUFS = 3
 FLOPS = 2 * (2 * EDGES) * D * H * 2
 
 
-def is_unit(unit):
-    return 0 <= unit < UNITS
-
-
-def starts_x_run(unit):
-    return is_unit(unit) and unit % X_RUN == 0
+def slot(slots, step):
+    return slots[step] if 0 <= step < len(slots) else None
 
 
 def ends_round(unit):
-    return is_unit(unit) and unit % SLICES == SLICES - 1
+    return unit is not None and unit % SLICES == SLICES - 1
 
 
 def ends_group(unit):
-    return is_unit(unit) and (unit % SLICES % GROUP_UNITS == GROUP_UNITS - 1 or ends_round(unit))
+    return unit is not None and (unit % SLICES % GROUP_UNITS == GROUP_UNITS - 1 or ends_round(unit))
 
 
 def tile_node_interaction_kernel(
@@ -112,16 +111,16 @@ def tile_node_interaction_kernel(
             x_tile = x_pool.tile([P, 2, D], BF16)
             x_tiles[rnd] = x_tile
 
-        def load_x_chunk(rnd, chunk):
+        def load_x_chunk(rnd, first, units):
             rows = slice(rnd * P, (rnd + 1) * P)
-            cols = slice(chunk * X_CHUNK, (chunk + 1) * X_CHUNK)
+            cols = slice(first * K_PASS, (first + units) * K_PASS)
             for half in range(2):
                 nc.sync.dma_start(out=x_tiles[rnd][:, half, cols], in_=x_halves[half][rows, cols])
 
         def load_x(rnd):
             new_x_tile(rnd)
-            for chunk in range(X_CHUNKS):
-                load_x_chunk(rnd, chunk)
+            for first in range(0, SLICES, 3):
+                load_x_chunk(rnd, first, min(3, SLICES - first))
 
         def load_scale_rows(plane, scale_rows):
             for quadrant in range(4):
@@ -139,29 +138,30 @@ def tile_node_interaction_kernel(
 
         new_x_tile(0)
         new_x_tile(1)
-        load_x_chunk(0, 0)
+        load_x_chunk(0, 0, 2)
         load_scale_rows(w1_scales, W1_scales.rearrange("g q n -> q g n"))
         nc.sync.dma_start(out=b1_row[0:1, :], in_=b1.rearrange("(o n) -> o n", o=1))
         nc.sync.dma_start(
             out=b2_rows[0:C_TILES, :].rearrange("c (a j) -> c a j", a=BLOCKS),
             in_=b2.rearrange("(a c j) -> c a j", a=BLOCKS, j=BLOCK),
         )
-        chunks_loaded = 1
+        x_loaded = 2
         for g in range(SLICES):
-            while chunks_loaded * X_CHUNK < (g + X_AHEAD) * K_PASS:
-                load_x_chunk(chunks_loaded // X_CHUNKS, chunks_loaded % X_CHUNKS)
-                chunks_loaded += 1
+            while x_loaded < min(g + X_LEAD, SLICES):
+                units = min(X_CHUNK_UNITS, SLICES - x_loaded)
+                load_x_chunk(0, x_loaded, units)
+                x_loaded += units
             nc.sync.dma_start(
                 out=w1_words[:, g, :].bitcast(I32),
                 in_=W1_words[g].rearrange("p n t -> p (n t)").bitcast(I32),
             )
-        nc.sync.dma_start(out=gate_rows[:], in_=x_edge_c.rearrange("(i p) h -> p i h", p=P))
-        while chunks_loaded < 2 * X_CHUNKS:
-            load_x_chunk(chunks_loaded // X_CHUNKS, chunks_loaded % X_CHUNKS)
-            chunks_loaded += 1
-        load_scale_rows(w2_scale_rows, W2_scales[0])
         w2_blocks = W2_words[0].rearrange("p n t -> p (n t)").bitcast(I32).rearrange("p (a m) -> p a m", a=BLOCKS)
         for chunk in range(W2_CHUNKS):
+            first = 3 * chunk
+            load_x_chunk(1, first, min(3, SLICES - first))
+            if chunk == 0:
+                nc.sync.dma_start(out=gate_rows[:], in_=x_edge_c.rearrange("(i p) h -> p i h", p=P))
+                load_scale_rows(w2_scale_rows, W2_scales[0])
             raw = w2_stage.tile([P, BLOCKS, CHUNK_TILES * BLOCK], I32)
             m_cols = slice(chunk * CHUNK_TILES * BLOCK, (chunk + 1) * CHUNK_TILES * BLOCK)
             nc.sync.dma_start(out=raw[:], in_=w2_blocks[:, :, m_cols])
@@ -208,25 +208,26 @@ def tile_node_interaction_kernel(
                     )
             xt_banks[unit] = xt_bank
 
-        def copy_x_run(first_unit, copy):
-            grouped = stream.tile([P, X_RUN, 2, P, PACK], BF16, align_bytes=64, tag="x_grouped")
-            for j in range(X_RUN):
-                copy(
+        def copy_x_run(units, copies):
+            first_unit = units[0]
+            grouped = stream.tile([P, len(units), 2, P, PACK], BF16, align_bytes=64, tag="x_grouped")
+            for j in range(len(units)):
+                copies[j](
                     out=grouped[:, j].bitcast(F32),
-                    in_=xt_banks[first_unit + j][:].rearrange("p a u r -> p a r u"),
+                    in_=xt_banks[units[j]][:].rearrange("p a u r -> p a r u"),
                 )
             x_grouped[first_unit] = grouped
 
-        def quantise_x_run(first_unit):
-            codes = stream.tile([P, X_RUN, 2 * P], U32, align_bytes=64, tag="x_codes")
-            scales = stream.tile([P, X_RUN, 2 * P], U8, align_bytes=64, tag="x_scales")
+        def quantise_x_run(units):
+            codes = stream.tile([P, len(units), 2 * P], U32, align_bytes=64, tag="x_codes")
+            scales = stream.tile([P, len(units), 2 * P], U8, align_bytes=64, tag="x_scales")
             nc.vector.quantize_mx(
                 out=codes[:].rearrange("p j r -> p (j r)").bitcast(FP8X4),
                 scales=scales[:].rearrange("p j r -> p (j r)"),
-                in_=x_grouped[first_unit][:].rearrange("p j a r t -> p (j a r t)"),
+                in_=x_grouped[units[0]][:].rearrange("p j a r t -> p (j a r t)"),
             )
-            for j in range(X_RUN):
-                x_codes[first_unit + j], x_scales[first_unit + j] = codes[:, j, :], scales[:, j, :]
+            for j in range(len(units)):
+                x_codes[units[j]], x_scales[units[j]] = codes[:, j, :], scales[:, j, :]
 
         def layer1(unit):
             rnd, g = divmod(unit, SLICES)
@@ -251,7 +252,8 @@ def tile_node_interaction_kernel(
                     out=biased[:, half, :], in0=sums1[rnd][half][:], in1=b1_all[:], op=ADD
                 )
             silu1 = per_round.tile([P, 2, H], F32, tag="silu1")
-            nc.scalar.activation(out=silu1[:], in_=biased[:], func=SILU)
+            for half in range(2):
+                nc.scalar.activation(out=silu1[:, half, :], in_=biased[:, half, :], func=SILU)
             activated[rnd] = silu1
 
         def gate(rnd):
@@ -276,7 +278,8 @@ def tile_node_interaction_kernel(
 
         def copy_h(rnd):
             grouped = per_round.tile([P, 2, P, PACK], BF16, align_bytes=64, tag="h_grouped")
-            nc.scalar.copy(out=grouped[:], in_=ht_banks[rnd][:].rearrange("p a t r -> p a r t"))
+            for half in range(2):
+                nc.scalar.copy(out=grouped[:, half], in_=ht_banks[rnd][:, half].rearrange("p t r -> p r t"))
             h_grouped[rnd] = grouped
 
         def quantise_h(rnd):
@@ -319,7 +322,7 @@ def tile_node_interaction_kernel(
                 )
             y_activated[unit] = silu
 
-        def add_halves(unit):
+        def add_halves(unit, engine):
             c = unit % SLICES
             first = unit - c % GROUP_UNITS
             if unit == first:
@@ -327,7 +330,7 @@ def tile_node_interaction_kernel(
                 total = stream.tile([P, BLOCKS, units * UNIT_TILES, BLOCK], F32, align_bytes=64, tag="total", bufs=TOTAL_BUFS)
                 totals[first] = total
             tiles = slice((unit - first) * UNIT_TILES, (unit - first + 1) * UNIT_TILES)
-            nc.gpsimd.tensor_tensor(
+            engine.tensor_tensor(
                 out=totals[first][:, :, tiles, :].rearrange("p b c i -> p c b i"),
                 in0=y_activated[unit][:, :, 0, :].rearrange("p c (b i) -> p c b i", b=BLOCKS),
                 in1=y_activated[unit][:, :, 1, :].rearrange("p c (b i) -> p c b i", b=BLOCKS),
@@ -351,36 +354,53 @@ def tile_node_interaction_kernel(
                     in_=turned[a * BLOCK : (a + 1) * BLOCK].rearrange("p b c j -> p b (c j)"),
                 )
 
+        def x_run(step):
+            if step < 0 or step % X_RUN:
+                return []
+            return [unit for unit in X_SLOTS[step : step + X_RUN] if unit is not None]
+
         for step in range(STEPS):
-            if ends_group(step - LAG_STORE):
-                turn_and_store(step - LAG_STORE)
-            if is_unit(step - LAG_SUM):
-                add_halves(step - LAG_SUM)
-            if is_unit(step - LAG_SILU2):
-                silu2(step - LAG_SILU2)
-            if is_unit(step - LAG_LAYER2):
-                layer2(step - LAG_LAYER2)
-            if ends_round(step - LAG_QUANTISE_H):
-                quantise_h((step - LAG_QUANTISE_H) // SLICES)
-            if ends_round(step - LAG_COPY_H):
-                copy_h((step - LAG_COPY_H) // SLICES)
-            if ends_round(step - LAG_TRANSPOSE_H):
-                transpose_h((step - LAG_TRANSPOSE_H) // SLICES)
-            if ends_round(step - LAG_GATE):
-                gate((step - LAG_GATE) // SLICES)
-            if ends_round(step - LAG_ACTIVATE1):
-                activate1((step - LAG_ACTIVATE1) // SLICES)
-            if is_unit(step - LAG_LAYER1):
-                layer1(step - LAG_LAYER1)
-            if starts_x_run(step - LAG_QUANTISE_X):
-                quantise_x_run(step - LAG_QUANTISE_X)
-            if starts_x_run(step - LAG_COPY_X):
-                copy_x_run(step - LAG_COPY_X, nc.scalar.copy if step < LAG_LAYER2 else nc.vector.tensor_copy)
-            if starts_x_run(step):
-                for unit in range(step, step + X_RUN):
-                    transpose_x(unit)
-                    if ends_round(unit) and unit // SLICES + 2 < ROUNDS:
-                        load_x(unit // SLICES + 2)
+            unit = slot(Y_SLOTS, step - LAG_SILU2)
+            if unit is not None:
+                silu2(unit)
+            unit = slot(Y_SLOTS, step)
+            if unit is not None:
+                layer2(unit)
+            unit = slot(X_SLOTS, step - LAG_ACTIVATE1)
+            if ends_round(unit):
+                activate1(unit // SLICES)
+            unit = slot(X_SLOTS, step - LAG_TRANSPOSE_H)
+            if ends_round(unit):
+                transpose_h(unit // SLICES)
+            unit = slot(X_SLOTS, step - LAG_COPY_H)
+            if ends_round(unit):
+                copy_h(unit // SLICES)
+            unit = slot(X_SLOTS, step - LAG_LAYER1)
+            if unit is not None:
+                layer1(unit)
+            units = x_run(step - LAG_QUANTISE_X)
+            if units:
+                quantise_x_run(units)
+            last_unit = slot(Y_SLOTS, step - LAG_STORE)
+            if ends_group(last_unit):
+                turn_and_store(last_unit)
+            unit = slot(Y_SLOTS, step - LAG_SUM)
+            if unit is not None:
+                add_halves(unit, nc.vector if unit >= UNITS - SLICES else nc.gpsimd)
+            units = x_run(step - LAG_COPY_X)
+            if units:
+                late = step >= LAG_LAYER2
+                copy_x_run(units, [nc.vector.tensor_copy if late and j not in SCALAR_COPIES else nc.scalar.copy for j in range(X_RUN)])
+            for unit in x_run(step):
+                transpose_x(unit)
+                if ends_round(unit) and unit // SLICES + 2 < ROUNDS:
+                    load_x(unit // SLICES + 2)
+            unit = slot(X_SLOTS, step - LAG_QUANTISE_H)
+            if ends_round(unit):
+                quantise_h(unit // SLICES)
+            unit = slot(X_SLOTS, step - LAG_GATE)
+            if ends_round(unit):
+                gate(unit // SLICES)
             if step == 1:
                 spread_b1()
                 turn_b2()

@@ -23,7 +23,7 @@ SLICES = D // K_PASS
 UNITS = ROUNDS * SLICES
 X_CHUNK_UNITS = 4
 X_RUN = 2
-SCALAR_COPIES = ()
+SCALAR_COPIES = (0,)
 BLOCK = 32
 BLOCKS = P // BLOCK
 C_TILES = D // P
@@ -35,8 +35,8 @@ STORE_ORDER = (0, 2, 1, 3)
 GROUP_UNITS = 2
 
 LAG_COPY_X = 1
-LAG_QUANTISE_X = 2
-LAG_LAYER1 = 3
+LAG_QUANTISE_X = 3
+LAG_LAYER1 = 4
 LAG_ACTIVATE1 = LAG_LAYER1 + 1
 LAG_GATE = LAG_LAYER1 + 1
 LAG_TRANSPOSE_H = LAG_LAYER1 + 2
@@ -146,26 +146,31 @@ def tile_node_interaction_kernel(
             in_=b2.rearrange("(a c j) -> c a j", a=BLOCKS, j=BLOCK),
         )
         x_loaded = 2
-        for g in range(SLICES):
-            while x_loaded < min(g + X_LEAD, SLICES):
-                units = min(X_CHUNK_UNITS, SLICES - x_loaded)
-                load_x_chunk(0, x_loaded, units)
+
+        def load_x_ahead(x_loaded, wanted):
+            while x_loaded < min(wanted, 2 * SLICES):
+                rnd, first = divmod(x_loaded, SLICES)
+                units = min(X_CHUNK_UNITS, SLICES - first)
+                load_x_chunk(rnd, first, units)
                 x_loaded += units
+            return x_loaded
+
+        for g in range(SLICES):
+            x_loaded = load_x_ahead(x_loaded, g + X_LEAD)
             nc.sync.dma_start(
                 out=w1_words[:, g, :].bitcast(I32),
                 in_=W1_words[g].rearrange("p n t -> p (n t)").bitcast(I32),
             )
+        nc.sync.dma_start(out=gate_rows[:], in_=x_edge_c.rearrange("(i p) h -> p i h", p=P))
+        load_scale_rows(w2_scale_rows, W2_scales[0])
         w2_blocks = W2_words[0].rearrange("p n t -> p (n t)").bitcast(I32).rearrange("p (a m) -> p a m", a=BLOCKS)
         for chunk in range(W2_CHUNKS):
-            first = 3 * chunk
-            load_x_chunk(1, first, min(3, SLICES - first))
-            if chunk == 0:
-                nc.sync.dma_start(out=gate_rows[:], in_=x_edge_c.rearrange("(i p) h -> p i h", p=P))
-                load_scale_rows(w2_scale_rows, W2_scales[0])
+            x_loaded = load_x_ahead(x_loaded, x_loaded + 1)
             raw = w2_stage.tile([P, BLOCKS, CHUNK_TILES * BLOCK], I32)
             m_cols = slice(chunk * CHUNK_TILES * BLOCK, (chunk + 1) * CHUNK_TILES * BLOCK)
             nc.sync.dma_start(out=raw[:], in_=w2_blocks[:, :, m_cols])
             w2_raw[chunk] = raw
+        load_x_ahead(x_loaded, 2 * SLICES)
 
         def spread_b1():
             spread = psum_2.tile([P, H], F32, tag="y")
@@ -219,8 +224,8 @@ def tile_node_interaction_kernel(
             x_grouped[first_unit] = grouped
 
         def quantise_x_run(units):
-            codes = stream.tile([P, len(units), 2 * P], U32, align_bytes=64, tag="x_codes")
-            scales = stream.tile([P, len(units), 2 * P], U8, align_bytes=64, tag="x_scales")
+            codes = stream.tile([P, len(units), 2 * P], U32, align_bytes=64, tag="x_codes", bufs=3)
+            scales = stream.tile([P, len(units), 2 * P], U8, align_bytes=64, tag="x_scales", bufs=3)
             nc.vector.quantize_mx(
                 out=codes[:].rearrange("p j r -> p (j r)").bitcast(FP8X4),
                 scales=scales[:].rearrange("p j r -> p (j r)"),
@@ -381,16 +386,16 @@ def tile_node_interaction_kernel(
             units = x_run(step - LAG_QUANTISE_X)
             if units:
                 quantise_x_run(units)
+            units = x_run(step - LAG_COPY_X)
+            if units:
+                late = step >= LAG_LAYER2
+                copy_x_run(units, [nc.vector.tensor_copy if late and j not in SCALAR_COPIES else nc.scalar.copy for j in range(X_RUN)])
             last_unit = slot(Y_SLOTS, step - LAG_STORE)
             if ends_group(last_unit):
                 turn_and_store(last_unit)
             unit = slot(Y_SLOTS, step - LAG_SUM)
             if unit is not None:
-                add_halves(unit, nc.vector if unit >= UNITS - SLICES else nc.gpsimd)
-            units = x_run(step - LAG_COPY_X)
-            if units:
-                late = step >= LAG_LAYER2
-                copy_x_run(units, [nc.vector.tensor_copy if late and j not in SCALAR_COPIES else nc.scalar.copy for j in range(X_RUN)])
+                add_halves(unit, nc.vector if unit >= UNITS - SLICES and unit % 3 == (UNITS - 1) % 3 else nc.gpsimd)
             for unit in x_run(step):
                 transpose_x(unit)
                 if ends_round(unit) and unit // SLICES + 2 < ROUNDS:

@@ -23,7 +23,7 @@ SLICES = D // K_PASS
 UNITS = ROUNDS * SLICES
 X_CHUNK_UNITS = 4
 X_RUN = 2
-SCALAR_COPIES = (0,)
+SCALAR_COPIES = (0, 1)
 BLOCK = 32
 BLOCKS = P // BLOCK
 C_TILES = D // P
@@ -395,7 +395,7 @@ def tile_node_interaction_kernel(
                 turn_and_store(last_unit)
             unit = slot(Y_SLOTS, step - LAG_SUM)
             if unit is not None:
-                add_halves(unit, nc.vector if unit >= UNITS - SLICES and unit % 3 == (UNITS - 1) % 3 else nc.gpsimd)
+                add_halves(unit, nc.vector)
             for unit in x_run(step):
                 transpose_x(unit)
                 if ends_round(unit) and unit // SLICES + 2 < ROUNDS:

@@ -54,7 +54,7 @@ SORT_W2_FROM = LAG_LAYER2 - 2
 X_LEAD = 4
 SILU_BUFS = 4
 TOTAL_BUFS = 2
-TURNED_BUFS = 3
+TURNED_BUFS = 5
 
 FLOPS = 2 * (2 * EDGES) * D * H * 2
 
@@ -67,8 +67,20 @@ def ends_round(unit):
     return unit is not None and unit % SLICES == SLICES - 1
 
 
+def by_tensor(unit):
+    return unit is not None and (unit >= UNITS - SLICES and (UNITS - 1 - unit) % 2 == 0)
+
+
+def group_of(unit):
+    if unit >= UNITS - SLICES - 0:
+        return unit, unit
+    c = unit % SLICES
+    first = unit - c % GROUP_UNITS
+    return first, min(first + GROUP_UNITS - 1, unit - c + SLICES - 1)
+
+
 def ends_group(unit):
-    return unit is not None and (unit % SLICES % GROUP_UNITS == GROUP_UNITS - 1 or ends_round(unit))
+    return unit is not None and not by_tensor(unit) and group_of(unit)[1] == unit
 
 
 def tile_node_interaction_kernel(
@@ -140,11 +152,6 @@ def tile_node_interaction_kernel(
         new_x_tile(1)
         load_x_chunk(0, 0, 2)
         load_scale_rows(w1_scales, W1_scales.rearrange("g q n -> q g n"))
-        nc.sync.dma_start(out=b1_row[0:1, :], in_=b1.rearrange("(o n) -> o n", o=1))
-        nc.sync.dma_start(
-            out=b2_rows[0:C_TILES, :].rearrange("c (a j) -> c a j", a=BLOCKS),
-            in_=b2.rearrange("(a c j) -> c a j", a=BLOCKS, j=BLOCK),
-        )
         x_loaded = 2
 
         def load_x_ahead(x_loaded, wanted):
@@ -161,6 +168,12 @@ def tile_node_interaction_kernel(
                 out=w1_words[:, g, :].bitcast(I32),
                 in_=W1_words[g].rearrange("p n t -> p (n t)").bitcast(I32),
             )
+            if g == 6:
+                nc.sync.dma_start(out=b1_row[0:1, :], in_=b1.rearrange("(o n) -> o n", o=1))
+                nc.sync.dma_start(
+                    out=b2_rows[0:C_TILES, :].rearrange("c (a j) -> c a j", a=BLOCKS),
+                    in_=b2.rearrange("(a c j) -> c a j", a=BLOCKS, j=BLOCK),
+                )
         nc.sync.dma_start(out=gate_rows[:], in_=x_edge_c.rearrange("(i p) h -> p i h", p=P))
         load_scale_rows(w2_scale_rows, W2_scales[0])
         w2_blocks = W2_words[0].rearrange("p n t -> p (n t)").bitcast(I32).rearrange("p (a m) -> p a m", a=BLOCKS)
@@ -202,7 +215,7 @@ def tile_node_interaction_kernel(
 
         def transpose_x(unit):
             rnd, g = divmod(unit, SLICES)
-            xt_bank = psum_t.tile([P, 2, 2, P], F32)
+            xt_bank = psum_t.tile([P, 2, 2, P], F32, tag="xt_bank")
             for half in range(2):
                 words = x_tiles[rnd][:, half, :].bitcast(F32)
                 for u in range(2):
@@ -328,10 +341,9 @@ def tile_node_interaction_kernel(
             y_activated[unit] = silu
 
         def add_halves(unit, engine):
-            c = unit % SLICES
-            first = unit - c % GROUP_UNITS
+            first, last = group_of(unit)
             if unit == first:
-                units = min(GROUP_UNITS, SLICES - c)
+                units = last - first + 1
                 total = stream.tile([P, BLOCKS, units * UNIT_TILES, BLOCK], F32, align_bytes=64, tag="total", bufs=TOTAL_BUFS)
                 totals[first] = total
             tiles = slice((unit - first) * UNIT_TILES, (unit - first + 1) * UNIT_TILES)
@@ -342,9 +354,34 @@ def tile_node_interaction_kernel(
                 op=ADD,
             )
 
+        def add_on_tensor(unit):
+            sum_bank = psum_t.tile([P, UNIT_TILES, P], F32, tag="xt_bank")
+            for tile in range(UNIT_TILES):
+                for half in range(2):
+                    nc.tensor.matmul(
+                        out=sum_bank[:, tile, :],
+                        lhsT=y_activated[unit][:, tile, half, :],
+                        rhs=ident_f32[:],
+                        is_transpose=True,
+                        start=(half == 0),
+                        stop=(half == 1),
+                    )
+            totals[unit] = sum_bank
+
+        def copy_and_store(unit):
+            rnd, c = divmod(unit, SLICES)
+            total = stream.tile([P, BLOCKS, UNIT_TILES, BLOCK], F32, align_bytes=64, tag="turned", bufs=TURNED_BUFS)
+            nc.vector.tensor_copy(
+                out=total[:].rearrange("r a c j -> r c a j"),
+                in_=totals[unit][:].rearrange("r c (a j) -> r c a j", a=BLOCKS),
+            )
+            out_blocks = out_rows[rnd * P : (rnd + 1) * P, :].rearrange("r (a n) -> r a n", a=BLOCKS)
+            cols = slice(c * UNIT_TILES * BLOCK, (c + 1) * UNIT_TILES * BLOCK)
+            nc.sync.dma_start(out=out_blocks[:, :, cols], in_=total[:].rearrange("r a c j -> r a (c j)"))
+
         def turn_and_store(last_unit):
             rnd, c = divmod(last_unit, SLICES)
-            first = last_unit - c % GROUP_UNITS
+            first = group_of(last_unit)[0]
             tiles = (last_unit - first + 1) * UNIT_TILES
             turned = stream.tile([P, BLOCKS, tiles, BLOCK], F32, align_bytes=64, tag="turned", bufs=TURNED_BUFS)
             nc.vector.transpose(
@@ -374,6 +411,13 @@ def tile_node_interaction_kernel(
             unit = slot(X_SLOTS, step - LAG_ACTIVATE1)
             if ends_round(unit):
                 activate1(unit // SLICES)
+            units = x_run(step - LAG_QUANTISE_X)
+            if units:
+                quantise_x_run(units)
+            units = x_run(step - LAG_COPY_X)
+            if units:
+                late = step >= LAG_LAYER2
+                copy_x_run(units, [nc.scalar.copy for j in range(X_RUN)])
             unit = slot(X_SLOTS, step - LAG_TRANSPOSE_H)
             if ends_round(unit):
                 transpose_h(unit // SLICES)
@@ -383,18 +427,15 @@ def tile_node_interaction_kernel(
             unit = slot(X_SLOTS, step - LAG_LAYER1)
             if unit is not None:
                 layer1(unit)
-            units = x_run(step - LAG_QUANTISE_X)
-            if units:
-                quantise_x_run(units)
-            units = x_run(step - LAG_COPY_X)
-            if units:
-                late = step >= LAG_LAYER2
-                copy_x_run(units, [nc.vector.tensor_copy if late and j not in SCALAR_COPIES else nc.scalar.copy for j in range(X_RUN)])
             last_unit = slot(Y_SLOTS, step - LAG_STORE)
+            if by_tensor(last_unit):
+                copy_and_store(last_unit)
             if ends_group(last_unit):
                 turn_and_store(last_unit)
             unit = slot(Y_SLOTS, step - LAG_SUM)
-            if unit is not None:
+            if by_tensor(unit):
+                add_on_tensor(unit)
+            elif unit is not None:
                 add_halves(unit, nc.vector)
             for unit in x_run(step):
                 transpose_x(unit)
@@ -406,7 +447,7 @@ def tile_node_interaction_kernel(
             unit = slot(X_SLOTS, step - LAG_GATE)
             if ends_round(unit):
                 gate(unit // SLICES)
-            if step == 1:
+            if step == 11:
                 spread_b1()
                 turn_b2()
             if step == SORT_W2_FROM:

@@ -51,6 +51,7 @@ X_SLOTS = list(range(SLICES)) + [None] * GAP + list(range(SLICES, UNITS))
 Y_SLOTS = [None] * LAG_LAYER2 + list(range(SLICES)) + [None] * GAP + list(range(SLICES, UNITS))
 STEPS = len(Y_SLOTS) + LAG_STORE
 SORT_W2_FROM = LAG_LAYER2 - 2
+W1_STARTS = (0, 2, 4, 6, 8, 10)
 X_LEAD = 4
 SILU_BUFS = 4
 TOTAL_BUFS = 2
@@ -112,6 +113,7 @@ def tile_node_interaction_kernel(
         gate_rows = keep.tile([P, ROUNDS, H], BF16)
         b1_row = keep.tile([P, H], BF16)
         b1_all = keep.tile([P, H], F32)
+        warm = keep.tile([P, 1], F32)
         b2_rows = keep.tile([P, P], BF16)
         b2_cols = keep.tile([P, C_TILES], F32)
 
@@ -145,6 +147,7 @@ def tile_node_interaction_kernel(
         nc.vector.memset(b1_row[:], 0.0)
         nc.vector.memset(b2_rows[:], 0.0)
         nc.vector.memset(w2_scale_rows[:].bitcast(I32), 0)
+        nc.scalar.activation(out=warm[:], in_=b1_row[:, 0:1], func=SILU)
         make_identity(nc, ident_f32[:])
         make_identity(nc, ident_bf16[:])
 
@@ -164,10 +167,12 @@ def tile_node_interaction_kernel(
 
         for g in range(SLICES):
             x_loaded = load_x_ahead(x_loaded, g + X_LEAD)
-            nc.sync.dma_start(
-                out=w1_words[:, g, :].bitcast(I32),
-                in_=W1_words[g].rearrange("p n t -> p (n t)").bitcast(I32),
-            )
+            if g in W1_STARTS:
+                groups = slice(g, min([s for s in W1_STARTS if s > g] + [SLICES]))
+                nc.sync.dma_start(
+                    out=w1_words[:, groups, :].bitcast(I32),
+                    in_=W1_words[groups].rearrange("g p n t -> p g (n t)").bitcast(I32),
+                )
             if g == 6:
                 nc.sync.dma_start(out=b1_row[0:1, :], in_=b1.rearrange("(o n) -> o n", o=1))
                 nc.sync.dma_start(
@@ -208,7 +213,7 @@ def tile_node_interaction_kernel(
             )
 
         def sort_w2(chunk):
-            nc.vector.tensor_copy(
+            (nc.vector if chunk == 0 else nc.gpsimd).tensor_copy(
                 out=w2_words[:, chunk * CHUNK_TILES : (chunk + 1) * CHUNK_TILES],
                 in_=w2_raw[chunk][:].rearrange("p a (c j) -> p c a j", j=BLOCK),
             )

from contextlib import ExitStack

import concourse.mybir as mybir
from concourse.masks import make_identity

F32 = mybir.dt.float32
BF16 = mybir.dt.bfloat16
I32 = mybir.dt.int32
U32 = mybir.dt.uint32
U8 = mybir.dt.uint8
FP8X4 = mybir.dt.float8_e4m3fn_x4
SILU = mybir.ActivationFunctionType.Silu
ADD = mybir.AluOpType.add
MULT = mybir.AluOpType.mult

P = 128
PACK = 4
K_PASS = P * PACK
EDGES, D, H = 512, 5632, 512
N_TILE = 512
ROUNDS = EDGES // P
SLICES = D // K_PASS
UNITS = ROUNDS * SLICES
X_CHUNK_UNITS = 4
X_RUN = 2
SCALAR_COPIES = (0, 1)
BLOCK = 32
BLOCKS = P // BLOCK
C_TILES = D // P
C_BLOCK = D // BLOCKS
UNIT_TILES = N_TILE // P
W2_CHUNKS = 4
CHUNK_TILES = C_TILES // W2_CHUNKS
STORE_ORDER = (0, 2, 1, 3)
GROUP_UNITS = 2

LAG_COPY_X = 1
LAG_QUANTISE_X = 3
LAG_LAYER1 = 4
LAG_ACTIVATE1 = LAG_LAYER1 + 1
LAG_GATE = LAG_LAYER1 + 1
LAG_TRANSPOSE_H = LAG_LAYER1 + 2
LAG_COPY_H = LAG_LAYER1 + 2
LAG_QUANTISE_H = LAG_LAYER1 + 2
LAG_LAYER2 = (SLICES - 1) + LAG_QUANTISE_H + 1
LAG_SILU2 = 1
LAG_SUM = 2
LAG_STORE = 3
GAP = 0
X_SLOTS = list(range(SLICES)) + [None] * GAP + list(range(SLICES, UNITS))
Y_SLOTS = [None] * LAG_LAYER2 + list(range(SLICES)) + [None] * GAP + list(range(SLICES, UNITS))
STEPS = len(Y_SLOTS) + LAG_STORE
SORT_W2_FROM = LAG_LAYER2 - 2
W1_STARTS = (0, 2, 4, 6, 8, 10)
X_LEAD = 4
SILU_BUFS = 4
TOTAL_BUFS = 2
TURNED_BUFS = 5

FLOPS = 2 * (2 * EDGES) * D * H * 2


def slot(slots, step):
    return slots[step] if 0 <= step < len(slots) else None


def ends_round(unit):
    return unit is not None and unit % SLICES == SLICES - 1


def by_tensor(unit):
    return unit is not None and (unit >= UNITS - SLICES and (UNITS - 1 - unit) % 2 == 0)


def group_of(unit):
    if unit >= UNITS - SLICES - 0:
        return unit, unit
    c = unit % SLICES
    first = unit - c % GROUP_UNITS
    return first, min(first + GROUP_UNITS - 1, unit - c + SLICES - 1)


def ends_group(unit):
    return unit is not None and not by_tensor(unit) and group_of(unit)[1] == unit


def tile_node_interaction_kernel(
    tc, node_embed, x_edge_c, ori, W1_words, W1_scales, b1, W2_words, W2_scales, b2, edge_num, out
):
    nc = tc.nc
    assert edge_num == EDGES
    x_halves = (node_embed, ori)
    out_rows = out.rearrange("e c d -> e (c d)")

    with ExitStack() as stack:
        stack.enter_context(tc.manual_schedule())
        keep = stack.enter_context(tc.tile_pool(name="keep", bufs=1))
        x_pool = stack.enter_context(tc.tile_pool(name="x_pool", bufs=2))
        w2_stage = stack.enter_context(tc.tile_pool(name="w2_stage", bufs=W2_CHUNKS))
        stream = stack.enter_context(tc.tile_pool(name="stream", bufs=3))
        per_round = stack.enter_context(tc.tile_pool(name="per_round", bufs=2))
        psum_t = stack.enter_context(tc.psum_pool(name="psum_t", bufs=2))
        psum_1 = stack.enter_context(tc.psum_pool(name="psum_1", bufs=1))
        psum_2 = stack.enter_context(tc.psum_pool(name="psum_2", bufs=4))

        ident_f32 = keep.tile([P, P], F32)
        ident_bf16 = keep.tile([P, P], BF16)
        w1_words = keep.tile([P, SLICES, PACK * H], U8, align_bytes=64)
        w1_scales = keep.tile([P, SLICES, H], U8, align_bytes=64)
        w2_words = keep.tile([P, C_TILES, BLOCKS, BLOCK], I32, align_bytes=64)
        w2_scale_rows = keep.tile([P, D], U8, align_bytes=64)
        w2_scales = keep.tile([P, C_TILES, BLOCKS, BLOCK // 4], I32, align_bytes=64)
        gate_rows = keep.tile([P, ROUNDS, H], BF16)
        b1_row = keep.tile([P, H], BF16)
        b1_all = keep.tile([P, H], F32)
        warm = keep.tile([P, 1], F32)
        b2_rows = keep.tile([P, P], BF16)
        b2_cols = keep.tile([P, C_TILES], F32)

        x_tiles, xt_banks, x_grouped, x_codes, x_scales = {}, {}, {}, {}, {}
        sums1, activated, h_sorted, ht_banks, h_grouped, h_codes, h_scales = {}, {}, {}, {}, {}, {}, {}
        w2_raw, y_banks, y_activated, totals = {}, {}, {}, {}

        def new_x_tile(rnd):
            x_tile = x_pool.tile([P, 2, D], BF16)
            x_tiles[rnd] = x_tile

        def load_x_chunk(rnd, first, units):
            rows = slice(rnd * P, (rnd + 1) * P)
            cols = slice(first * K_PASS, (first + units) * K_PASS)
            for half in range(2):
                nc.sync.dma_start(out=x_tiles[rnd][:, half, cols], in_=x_halves[half][rows, cols])

        def load_x(rnd):
            new_x_tile(rnd)
            for first in range(0, SLICES, 3):
                load_x_chunk(rnd, first, min(3, SLICES - first))

        def load_scale_rows(plane, scale_rows):
            for quadrant in range(4):
                nc.sync.dma_start(
                    out=plane[32 * quadrant : 32 * quadrant + 4].bitcast(I32),
                    in_=scale_rows[4 * quadrant : 4 * quadrant + 4].bitcast(I32),
                )

        nc.vector.memset(w1_scales[:].bitcast(I32), 0)
        nc.vector.memset(b1_row[:], 0.0)
        nc.vector.memset(b2_rows[:], 0.0)
        nc.vector.memset(w2_scale_rows[:].bitcast(I32), 0)
        nc.scalar.activation(out=warm[:], in_=b1_row[:, 0:1], func=SILU)
        make_identity(nc, ident_f32[:])
        make_identity(nc, ident_bf16[:])

        new_x_tile(0)
        new_x_tile(1)
        load_x_chunk(0, 0, 2)
        load_scale_rows(w1_scales, W1_scales.rearrange("g q n -> q g n"))
        x_loaded = 2

        def load_x_ahead(x_loaded, wanted):
            while x_loaded < min(wanted, 2 * SLICES):
                rnd, first = divmod(x_loaded, SLICES)
                units = min(X_CHUNK_UNITS, SLICES - first)
                load_x_chunk(rnd, first, units)
                x_loaded += units
            return x_loaded

        for g in range(SLICES):
            x_loaded = load_x_ahead(x_loaded, g + X_LEAD)
            if g in W1_STARTS:
                groups = slice(g, min([s for s in W1_STARTS if s > g] + [SLICES]))
                nc.sync.dma_start(
                    out=w1_words[:, groups, :].bitcast(I32),
                    in_=W1_words[groups].rearrange("g p n t -> p g (n t)").bitcast(I32),
                )
            if g == 6:
                nc.sync.dma_start(out=b1_row[0:1, :], in_=b1.rearrange("(o n) -> o n", o=1))
                nc.sync.dma_start(
                    out=b2_rows[0:C_TILES, :].rearrange("c (a j) -> c a j", a=BLOCKS),
                    in_=b2.rearrange("(a c j) -> c a j", a=BLOCKS, j=BLOCK),
                )
        nc.sync.dma_start(out=gate_rows[:], in_=x_edge_c.rearrange("(i p) h -> p i h", p=P))
        load_scale_rows(w2_scale_rows, W2_scales[0])
        w2_blocks = W2_words[0].rearrange("p n t -> p (n t)").bitcast(I32).rearrange("p (a m) -> p a m", a=BLOCKS)
        for chunk in range(W2_CHUNKS):
            x_loaded = load_x_ahead(x_loaded, x_loaded + 1)
            raw = w2_stage.tile([P, BLOCKS, CHUNK_TILES * BLOCK], I32)
            m_cols = slice(chunk * CHUNK_TILES * BLOCK, (chunk + 1) * CHUNK_TILES * BLOCK)
            nc.sync.dma_start(out=raw[:], in_=w2_blocks[:, :, m_cols])
            w2_raw[chunk] = raw
        load_x_ahead(x_loaded, 2 * SLICES)

        def spread_b1():
            spread = psum_2.tile([P, H], F32, tag="y")
            nc.tensor.matmul(
                out=spread[:],
                lhsT=ident_bf16[:, 0:1].to_broadcast([P, P]),
                rhs=b1_row[:],
                start=True,
                stop=True,
            )
            nc.vector.tensor_copy(out=b1_all[:], in_=spread[:])

        def turn_b2():
            turned = psum_2.tile([P, P], BF16, tag="y")
            nc.tensor.transpose(out=turned[:], in_=b2_rows[:], identity=ident_bf16[:])
            nc.vector.tensor_copy(out=b2_cols[:], in_=turned[:, 0:C_TILES])

        def sort_w2_scales():
            nc.vector.tensor_copy(
                out=w2_scales[:],
                in_=w2_scale_rows[:].bitcast(I32).rearrange("p (a c j) -> p c a j", a=BLOCKS, c=C_TILES),
            )

        def sort_w2(chunk):
            (nc.vector if chunk == 0 else nc.gpsimd).tensor_copy(
                out=w2_words[:, chunk * CHUNK_TILES : (chunk + 1) * CHUNK_TILES],
                in_=w2_raw[chunk][:].rearrange("p a (c j) -> p c a j", j=BLOCK),
            )

        def transpose_x(unit):
            rnd, g = divmod(unit, SLICES)
            xt_bank = psum_t.tile([P, 2, 2, P], F32, tag="xt_bank")
            for half in range(2):
                words = x_tiles[rnd][:, half, :].bitcast(F32)
                for u in range(2):
                    nc.tensor.transpose(
                        out=xt_bank[:, half, u, :],
                        in_=words[:, g * 2 * P + u : (g + 1) * 2 * P : 2],
                        identity=ident_f32[:],
                    )
            xt_banks[unit] = xt_bank

        def copy_x_run(units, copies):
            first_unit = units[0]
            grouped = stream.tile([P, len(units), 2, P, PACK], BF16, align_bytes=64, tag="x_grouped")
            for j in range(len(units)):
                copies[j](
                    out=grouped[:, j].bitcast(F32),
                    in_=xt_banks[units[j]][:].rearrange("p a u r -> p a r u"),
                )
            x_grouped[first_unit] = grouped

        def quantise_x_run(units):
            codes = stream.tile([P, len(units), 2 * P], U32, align_bytes=64, tag="x_codes", bufs=3)
            scales = stream.tile([P, len(units), 2 * P], U8, align_bytes=64, tag="x_scales", bufs=3)
            nc.vector.quantize_mx(
                out=codes[:].rearrange("p j r -> p (j r)").bitcast(FP8X4),
                scales=scales[:].rearrange("p j r -> p (j r)"),
                in_=x_grouped[units[0]][:].rearrange("p j a r t -> p (j a r t)"),
            )
            for j in range(len(units)):
                x_codes[units[j]], x_scales[units[j]] = codes[:, j, :], scales[:, j, :]

        def layer1(unit):
            rnd, g = divmod(unit, SLICES)
            if g == 0:
                sums1[rnd] = [psum_1.tile([P, H], F32, name="sum1_half%d" % half) for half in range(2)]
            for half in range(2):
                rows = slice(half * P, (half + 1) * P)
                nc.tensor.matmul_mx(
                    out=sums1[rnd][half][:],
                    lhsT=x_codes[unit][:, rows].bitcast(FP8X4),
                    lhsT_scale=x_scales[unit][:, rows],
                    rhs=w1_words[:, g, :].bitcast(FP8X4),
                    rhs_scale=w1_scales[:, g, :],
                    start=(g == 0),
                    stop=(g == SLICES - 1),
                )

        def activate1(rnd):
            biased = per_round.tile([P, 2, H], F32, tag="biased1")
            for half in range(2):
                nc.vector.tensor_tensor(
                    out=biased[:, half, :], in0=sums1[rnd][half][:], in1=b1_all[:], op=ADD
                )
            silu1 = per_round.tile([P, 2, H], F32, tag="silu1")
            for half in range(2):
                nc.scalar.activation(out=silu1[:, half, :], in_=biased[:, half, :], func=SILU)
            activated[rnd] = silu1

        def gate(rnd):
            h_tile = per_round.tile([P, 2, PACK, P], BF16, tag="h_sorted")
            for half in range(2):
                nc.vector.tensor_tensor(
                    out=h_tile[:, half],
                    in0=activated[rnd][:, half, :].rearrange("r (p t) -> r t p", t=PACK),
                    in1=gate_rows[:, rnd, :].rearrange("r (p t) -> r t p", t=PACK),
                    op=MULT,
                )
            h_sorted[rnd] = h_tile

        def transpose_h(rnd):
            ht_bank = psum_2.tile([P, 2, PACK, P], BF16, tag="y")
            for half in range(2):
                for t in range(PACK):
                    nc.tensor.transpose(
                        out=ht_bank[:, half, t, :], in_=h_sorted[rnd][:, half, t, :], identity=ident_bf16[:]
                    )
            ht_banks[rnd] = ht_bank

        def copy_h(rnd):
            grouped = per_round.tile([P, 2, P, PACK], BF16, align_bytes=64, tag="h_grouped")
            for half in range(2):
                nc.scalar.copy(out=grouped[:, half], in_=ht_banks[rnd][:, half].rearrange("p t r -> p r t"))
            h_grouped[rnd] = grouped

        def quantise_h(rnd):
            codes = per_round.tile([P, 2 * P], U32, align_bytes=64, tag="h_codes")
            scales = per_round.tile([P, 2 * P], U8, align_bytes=64, tag="h_scales")
            nc.vector.quantize_mx(
                out=codes[:].bitcast(FP8X4),
                scales=scales[:],
                in_=h_grouped[rnd][:].rearrange("p a r t -> p (a r t)"),
            )
            h_codes[rnd], h_scales[rnd] = codes, scales

        def layer2(unit):
            rnd, c = divmod(unit, SLICES)
            y_banks[unit] = [
                psum_2.tile([P, 2, 2 * P], F32, name="y_pair%d" % pair, tag="y") for pair in range(UNIT_TILES // 2)
            ]
            for tile in range(UNIT_TILES):
                c_tile = c * UNIT_TILES + tile
                nc.tensor.matmul_mx(
                    out=y_banks[unit][tile // 2][:, tile % 2, :],
                    lhsT=w2_words[:, c_tile].rearrange("p a j -> p (a j)").bitcast(FP8X4),
                    lhsT_scale=w2_scales[:, c_tile].rearrange("p a j -> p (a j)").bitcast(U8),
                    rhs=h_codes[rnd][:].bitcast(FP8X4),
                    rhs_scale=h_scales[rnd][:],
                    start=True,
                    stop=True,
                )

        def silu2(unit):
            c = unit % SLICES
            silu = stream.tile([P, UNIT_TILES, 2, P], F32, tag="silu2", bufs=SILU_BUFS)
            for tile in range(UNIT_TILES):
                c_tile = c * UNIT_TILES + tile
                nc.scalar.activation(
                    out=silu[:, tile].rearrange("p a r -> p (a r)"),
                    in_=y_banks[unit][tile // 2][:, tile % 2, :],
                    func=SILU,
                    bias=b2_cols[:, c_tile : c_tile + 1],
                )
            y_activated[unit] = silu

        def add_halves(unit, engine):
            first, last = group_of(unit)
            if unit == first:
                units = last - first + 1
                total = stream.tile([P, BLOCKS, units * UNIT_TILES, BLOCK], F32, align_bytes=64, tag="total", bufs=TOTAL_BUFS)
                totals[first] = total
            tiles = slice((unit - first) * UNIT_TILES, (unit - first + 1) * UNIT_TILES)
            engine.tensor_tensor(
                out=totals[first][:, :, tiles, :].rearrange("p b c i -> p c b i"),
                in0=y_activated[unit][:, :, 0, :].rearrange("p c (b i) -> p c b i", b=BLOCKS),
                in1=y_activated[unit][:, :, 1, :].rearrange("p c (b i) -> p c b i", b=BLOCKS),
                op=ADD,
            )

        def add_on_tensor(unit):
            sum_bank = psum_t.tile([P, UNIT_TILES, P], F32, tag="xt_bank")
            for tile in range(UNIT_TILES):
                for half in range(2):
                    nc.tensor.matmul(
                        out=sum_bank[:, tile, :],
                        lhsT=y_activated[unit][:, tile, half, :],
                        rhs=ident_f32[:],
                        is_transpose=True,
                        start=(half == 0),
                        stop=(half == 1),
                    )
            totals[unit] = sum_bank

        def copy_and_store(unit):
            rnd, c = divmod(unit, SLICES)
            total = stream.tile([P, BLOCKS, UNIT_TILES, BLOCK], F32, align_bytes=64, tag="turned", bufs=TURNED_BUFS)
            nc.vector.tensor_copy(
                out=total[:].rearrange("r a c j -> r c a j"),
                in_=totals[unit][:].rearrange("r c (a j) -> r c a j", a=BLOCKS),
            )
            out_blocks = out_rows[rnd * P : (rnd + 1) * P, :].rearrange("r (a n) -> r a n", a=BLOCKS)
            cols = slice(c * UNIT_TILES * BLOCK, (c + 1) * UNIT_TILES * BLOCK)
            nc.sync.dma_start(out=out_blocks[:, :, cols], in_=total[:].rearrange("r a c j -> r a (c j)"))

        def turn_and_store(last_unit):
            rnd, c = divmod(last_unit, SLICES)
            first = group_of(last_unit)[0]
            tiles = (last_unit - first + 1) * UNIT_TILES
            turned = stream.tile([P, BLOCKS, tiles, BLOCK], F32, align_bytes=64, tag="turned", bufs=TURNED_BUFS)
            nc.vector.transpose(
                out=turned[:].rearrange("p b c j -> p (b c j)"),
                in_=totals[first][:].rearrange("p b c i -> p (b c i)"),
            )
            first_col = first % SLICES * UNIT_TILES * BLOCK
            for a in STORE_ORDER:
                cols = slice(a * C_BLOCK + first_col, a * C_BLOCK + first_col + tiles * BLOCK)
                nc.sync.dma_start(
                    out=out_rows[rnd * P : (rnd + 1) * P, cols].rearrange("(b i) n -> i b n", i=BLOCK),
                    in_=turned[a * BLOCK : (a + 1) * BLOCK].rearrange("p b c j -> p b (c j)"),
                )

        def x_run(step):
            if step < 0 or step % X_RUN:
                return []
            return [unit for unit in X_SLOTS[step : step + X_RUN] if unit is not None]

        for step in range(STEPS):
            unit = slot(Y_SLOTS, step - LAG_SILU2)
            if unit is not None:
                silu2(unit)
            unit = slot(Y_SLOTS, step)
            if unit is not None:
                layer2(unit)
            unit = slot(X_SLOTS, step - LAG_ACTIVATE1)
            if ends_round(unit):
                activate1(unit // SLICES)
            units = x_run(step - LAG_QUANTISE_X)
            if units:
                quantise_x_run(units)
            units = x_run(step - LAG_COPY_X)
            if units:
                late = step >= LAG_LAYER2
                copy_x_run(units, [nc.scalar.copy for j in range(X_RUN)])
            unit = slot(X_SLOTS, step - LAG_TRANSPOSE_H)
            if ends_round(unit):
                transpose_h(unit // SLICES)
            unit = slot(X_SLOTS, step - LAG_COPY_H)
            if ends_round(unit):
                copy_h(unit // SLICES)
            unit = slot(X_SLOTS, step - LAG_LAYER1)
            if unit is not None:
                layer1(unit)
            last_unit = slot(Y_SLOTS, step - LAG_STORE)
            if by_tensor(last_unit):
                copy_and_store(last_unit)
            if ends_group(last_unit):
                turn_and_store(last_unit)
            unit = slot(Y_SLOTS, step - LAG_SUM)
            if by_tensor(unit):
                add_on_tensor(unit)
            elif unit is not None:
                add_halves(unit, nc.vector)
            for unit in x_run(step):
                transpose_x(unit)
                if ends_round(unit) and unit // SLICES + 2 < ROUNDS:
                    load_x(unit // SLICES + 2)
            unit = slot(X_SLOTS, step - LAG_QUANTISE_H)
            if ends_round(unit):
                quantise_h(unit // SLICES)
            unit = slot(X_SLOTS, step - LAG_GATE)
            if ends_round(unit):
                gate(unit // SLICES)
            if step == 11:
                spread_b1()
                turn_b2()
            if step == SORT_W2_FROM:
                sort_w2_scales()
            for chunk in range(W2_CHUNKS):
                if step == SORT_W2_FROM + 2 * chunk:
                    sort_w2(chunk)
